import numpy as np
import ml_dtypes


def mxq(x, axis, fmt="e4m3"):
    dtype, down = {"e4m3": (ml_dtypes.float8_e4m3fn, 7), "e5m2": (ml_dtypes.float8_e5m2, 14)}[fmt]
    v = np.moveaxis(np.asarray(x, np.float32).astype(ml_dtypes.bfloat16).astype(np.float64), axis, -1)
    blocks = v.reshape(v.shape[:-1] + (-1, 32))
    amax = np.abs(blocks).max(-1, keepdims=True)
    byte = np.maximum(np.where(amax > 0, np.frexp(amax)[1] - 1 + 127, 0) - down, 1)
    scale = np.exp2(byte - 127.0)
    codes = (blocks / scale).astype(np.float32).astype(dtype).astype(np.float64)
    return np.moveaxis((codes * scale).reshape(v.shape), -1, axis)


WIDE = False


def mx_kscale(k):
    if not WIDE:
        return np.ones(k)
    levels = np.array([10, -10, 5, -5, 0])
    a = np.random.permutation(np.resize(levels, k // 512 * 4)).reshape(k // 512, 4)
    idx = np.arange(k)
    return np.exp2(a[idx // 512, idx % 128 // 32])


BF16 = ml_dtypes.bfloat16


def bf(x):
    return np.asarray(x, np.float32).astype(BF16)


def f64(x):
    return np.asarray(x).astype(np.float64)


B, T, P, F, G, R, C, O = 1024, 8, 768, 256, 512, 128, 4, 10


def setup_inputs():
    s, t = mx_kscale(P + F), mx_kscale(G)
    u = np.roll(t, R)
    r0 = np.concatenate([1.0 / (np.sqrt(P + F) * s), [0.1]])[:, None]
    r1 = np.concatenate([1.5 / (np.sqrt(G) * t), [0.1]])[:, None]
    return {"primary_input": bf((np.random.standard_normal((B, T, P)) * s[:P]).reshape(B, T * P)),
            "prev": bf((np.maximum(np.random.standard_normal((B, T, F)), 0.0) * 0.9 * s[P:]).reshape(B, T * F)),
            "col": bf(np.array([float(np.random.randint(1, C))])),
            "W0": bf(np.random.standard_normal((P + F + 1, G)) * r0 * u),
            "b0": bf(np.random.standard_normal(G) * 0.2 * u),
            "W1": bf(np.random.standard_normal((G + 1, F)) * r1),
            "b1": bf(np.random.standard_normal(F) * 0.2)}


def reference(primary_input, prev, col, W0, b0, W1, b1):
    w0, w1, c = f64(W0), f64(W1), f64(col)
    inp = np.concatenate([f64(primary_input).reshape(B, T, P), f64(prev).reshape(B, T, F)], axis=-1)
    a = (mxq(inp, 2, "e4m3") @ mxq(w0[:P + F], 0, "e4m3")) + c * w0[P + F] + f64(b0)
    h = np.roll(np.maximum(a, 0.0).reshape(B, T * G), -R, axis=1).reshape(B, T, G)
    y = (mxq(h, 2, "e4m3") @ mxq(w1[:G], 0, "e4m3")) + c * w1[G] + f64(b1)
    return np.roll(np.maximum(y, 0.0).reshape(B, T * F), R, axis=1)

@@ -1,0 +1,244 @@
+from contextlib import ExitStack
+
+import concourse.mybir as mybir
+from concourse.masks import make_identity
+
+F32 = mybir.dt.float32
+BF16 = mybir.dt.bfloat16
+U32 = mybir.dt.uint32
+U8 = mybir.dt.uint8
+FP8X4 = mybir.dt.float8_e4m3fn_x4
+ACT = mybir.ActivationFunctionType
+ALU = mybir.AluOpType
+
+P = 128
+B, T, PK, F, G = 1024, 8, 768, 256, 512
+NCH = 2 * (B // P)
+FLOPS = 2 * B * T * ((PK + F) * G + G * F)
+PINNED = True
+GPSIMD_RELU_BELOW = 0
+SCALAR_RELU_FROM = 99
+BT, BA, BY = 3, 3, 2
+
+
+def tile_capsuleneuralnetwork_pa_t_kernel(tc, primary_input, prev, col, W0, b0, W1, b1, out):
+    nc = tc.nc
+    with ExitStack() as ctx:
+        if PINNED:
+            ctx.enter_context(tc.manual_schedule())
+        const = ctx.enter_context(tc.tile_pool(name="const", bufs=1))
+        xpool = ctx.enter_context(tc.tile_pool(name="xpool", bufs=8))
+        work = ctx.enter_context(tc.tile_pool(name="work", bufs=3))
+        psum = ctx.enter_context(tc.psum_pool(name="psum", bufs=1))
+
+        xp_t, xv_t, gx_t, xq_t, xs_t, ht_t, gh_t, hq_t, hs_t, y_t = {}, {}, {}, {}, {}, {}, {}, {}, {}, {}
+
+        def load(k):
+            i, c = divmod(k, 2)
+            rows = slice(P * i, P * i + P)
+            xp = xpool.tile([P, 4 * PK], BF16, tag="xp", name="xp")
+            nc.sync.dma_start(out=xp[:], in_=primary_input[rows, 4 * PK * c : 4 * PK * (c + 1)])
+            xv = xpool.tile([P, 4 * F], BF16, tag="xv", name="xv")
+            nc.sync.dma_start(out=xv[:], in_=prev[rows, 4 * F * c : 4 * F * (c + 1)])
+            xp_t[k], xv_t[k] = xp, xv
+
+        w0raw = const.tile([P, 4 * 2 * G], BF16)
+
+        nc.sync.dma_start(
+            out=w0raw[:].rearrange("p (a r) -> p a r", a=4),
+            in_=W0[0 : PK + F, :].rearrange("(a p e) n -> p a (e n)", a=4, e=2),
+        )
+        load(0)
+        load(1)
+
+        c1 = const.tile([1, 1], BF16)
+        nc.scalar.dma_start(out=c1[:], in_=col.rearrange("(a b) -> a b", a=1))
+        wb0 = const.tile([P, G], BF16)
+        wb1 = const.tile([P, F], BF16)
+        colones = const.tile([P, P], BF16)
+        nc.vector.memset(wb0[:], 0.0)
+        nc.vector.memset(wb1[:], 0.0)
+        nc.vector.memset(colones[:], 0.0)
+        nc.vector.memset(colones[32:33, :], 1.0)
+        nc.scalar.dma_start(out=wb0[0:1, :], in_=W0[PK + F : PK + F + 1, :])
+        nc.scalar.dma_start(out=wb0[32:33, :], in_=b0.rearrange("(o n) -> o n", o=1))
+        nc.scalar.dma_start(out=wb1[0:1, :], in_=W1[G : G + 1, :])
+        nc.scalar.dma_start(out=wb1[32:33, :], in_=b1.rearrange("(o n) -> o n", o=1))
+        w1raw = const.tile([P, 4 * F], BF16)
+        nc.scalar.dma_start(
+            out=w1raw[:].rearrange("p (s f) -> p s f", s=4),
+            in_=W1[0:G, :].rearrange("(s p) f -> p s f", p=P),
+        )
+        nc.vector.tensor_copy(out=colones[0:1, :], in_=c1[0:1, 0:1].to_broadcast([1, P]))
+
+        ident = const.tile([P, P], F32)
+        make_identity(nc, ident[:])
+
+        w0g = const.tile([P, 2 * G * 4], BF16, align_bytes=64)
+        w0q = const.tile([P, 2 * G], U32, align_bytes=64)
+        w0s = const.tile([P, 2 * G], U8, align_bytes=64)
+        for g in range(2):
+            nc.vector.tensor_copy(
+                out=w0g[:, 4 * G * g : 4 * G * (g + 1)].rearrange("p (c i t) -> p c t i", i=4, t=4),
+                in_=w0raw[:, 4 * G * g : 4 * G * (g + 1)].rearrange("p (t c i) -> p c t i", t=4, i=4),
+            )
+        w1g = const.tile([P, F * 4], BF16, align_bytes=64)
+        w1q = const.tile([P, F], U32, align_bytes=64)
+        w1s = const.tile([P, F], U8, align_bytes=64)
+        nc.vector.tensor_copy(
+            out=w1g[:].rearrange("p (c i t) -> p c t i", i=4, t=4),
+            in_=w1raw[:].rearrange("p (t c i) -> p c t i", t=4, i=4),
+        )
+        nc.vector.quantize_mx(out=w0q[:].bitcast(FP8X4), scales=w0s[:], in_=w0g[:])
+        nc.vector.quantize_mx(out=w1q[:].bitcast(FP8X4), scales=w1s[:], in_=w1g[:])
+
+        bias1 = const.tile([P, 2 * F], F32)
+        bias0 = const.tile([P, 4], F32)
+
+        def biases():
+            pb1 = psum.tile([P, 512], F32, tag="Y", bufs=BY, name="pb1")
+            for r in range(2):
+                nc.tensor.matmul(out=pb1[:, F * r : F * (r + 1)], lhsT=colones[:], rhs=wb1[:], start=True, stop=True)
+            nc.vector.tensor_copy(out=bias1[:], in_=pb1[:])
+            pb0 = psum.tile([P, 512], F32, tag="Y", bufs=BY, name="pb0")
+            for m in range(4):
+                nc.tensor.matmul(
+                    out=pb0[:, 32 * m : 32 * (m + 1)], lhsT=wb0[:, P * m : P * (m + 1)], rhs=colones[:, 0:32],
+                    start=True, stop=True,
+                )
+            nc.vector.tensor_copy(out=bias0[:], in_=pb0[:, 0:128].rearrange("p (m n) -> p m n", m=4)[:, :, 0])
+
+        def tr(k):
+            xpw = xp_t[k][:].bitcast(F32)
+            xvw = xv_t[k][:].bitcast(F32)
+            gx = work.tile([P, 4096], BF16, tag="gx", name="gx", align_bytes=64)
+            gxw = gx[:].bitcast(F32).rearrange("p (g n u) -> p g n u", g=2, u=2)
+            for g in range(2):
+                for h in range(2):
+                    tp = psum.tile([P, 512], F32, tag="T", bufs=BT, name="tp")
+                    tpv = tp[:].rearrange("p (t u b) -> p t u b", t=2, u=2)
+                    for tt in range(2):
+                        tl = 2 * h + tt
+                        for u in range(2):
+                            if g == 1 and u == 1:
+                                src = xvw[:, 128 * tl : 128 * tl + 128]
+                            else:
+                                w = 384 * tl + 256 * g + 128 * u
+                                src = xpw[:, w : w + 128]
+                            nc.tensor.transpose(tpv[:, tt, u, :], src, ident[:])
+                    nc.scalar.copy(
+                        out=gxw[:, g, 256 * h : 256 * h + 256, :].rearrange("p (t b) u -> p t b u", t=2),
+                        in_=tpv.rearrange("p t u b -> p t b u"),
+                    )
+            gx_t[k] = gx
+
+        def qx(k):
+            xq = work.tile([P, 1024], U32, tag="xq", name="xq", align_bytes=64)
+            xs = work.tile([P, 1024], U8, tag="xs", name="xs", align_bytes=64)
+            nc.vector.quantize_mx(out=xq[:].bitcast(FP8X4), scales=xs[:], in_=gx_t[k][:])
+            xq_t[k], xs_t[k] = xq, xs
+
+        def l1(k):
+            i, c = divmod(k, 2)
+            if c == 0:
+                ht_t[i] = work.tile([P, 4096], BF16, tag="ht", name="ht")
+            htv = ht_t[i][:].rearrange("p (s n) -> p s n", s=4)
+            xq, xs = xq_t[k], xs_t[k]
+            for m in range(4):
+                acc = psum.tile([P, 512], F32, tag="A", bufs=BA, name="acc")
+                for g in range(2):
+                    wc = slice(G * g + P * m, G * g + P * m + P)
+                    xc = slice(512 * g, 512 * g + 512)
+                    nc.tensor.matmul_mx(
+                        out=acc[:],
+                        lhsT=w0q[:, wc].bitcast(FP8X4), lhsT_scale=w0s[:, wc],
+                        rhs=xq[:, xc].bitcast(FP8X4), rhs_scale=xs[:, xc],
+                        start=(g == 0), stop=(g == 1),
+                    )
+                bias = bias0[:, m : m + 1]
+                if m > 0:
+                    pieces = [(0, 512, m - 1, 512 * c)]
+                elif c == 0:
+                    pieces = [(0, 128, 3, 896), (128, 512, 3, 0)]
+                else:
+                    pieces = [(0, 512, 3, 384)]
+                for lo, hi, s, dst in pieces:
+                    nc.scalar.activation(
+                        out=htv[:, s, dst : dst + hi - lo], in_=acc[:, lo:hi], func=ACT.Relu, bias=bias, scale=1.0
+                    )
+
+        def rg(k):
+            i, c = divmod(k, 2)
+            htv = ht_t[i][:].rearrange("p (s n) -> p s n", s=4)
+            gh = work.tile([P, 2048], BF16, tag="gh", name="gh", align_bytes=64)
+            nc.vector.tensor_copy(
+                out=gh[:].rearrange("p (c i s) -> p c s i", i=4, s=4),
+                in_=htv[:, :, 512 * c : 512 * c + 512].rearrange("p s (c i) -> p c s i", i=4),
+            )
+            gh_t[k] = gh
+
+        def qh(k):
+            hq = work.tile([P, 512], U32, tag="hq", name="hq", align_bytes=64)
+            hs = work.tile([P, 512], U8, tag="hs", name="hs", align_bytes=64)
+            nc.vector.quantize_mx(out=hq[:].bitcast(FP8X4), scales=hs[:], in_=gh_t[k][:])
+            hq_t[k], hs_t[k] = hq, hs
+
+        def l2(k):
+            hq, hs = hq_t[k], hs_t[k]
+            ys = []
+            for j in range(2):
+                y = psum.tile([P, 512], F32, tag="Y", bufs=BY, name="y")
+                for tt in range(2):
+                    hc = slice(P * (2 * j + tt), P * (2 * j + tt) + P)
+                    nc.tensor.matmul_mx(
+                        out=y[:, F * tt : F * (tt + 1)],
+                        lhsT=hq[:, hc].bitcast(FP8X4), lhsT_scale=hs[:, hc],
+                        rhs=w1q[:].bitcast(FP8X4), rhs_scale=w1s[:],
+                        start=True, stop=True,
+                    )
+                ys.append(y)
+            y_t[k] = ys
+
+        def yadd(k):
+            i, c = divmod(k, 2)
+            rows = slice(P * i, P * i + P)
+            osb = work.tile([P, 1024], F32, tag="osb", bufs=4, name="osb")
+            for j in range(2):
+                nc.vector.tensor_tensor(
+                    out=osb[:, 512 * j : 512 * (j + 1)], in0=y_t[k][j][:], in1=bias1[:], op=ALU.add
+                )
+            if k < GPSIMD_RELU_BELOW:
+                nc.gpsimd.tensor_scalar(
+                    out=osb[:], in0=osb[:], scalar1=3.0e38, scalar2=0.0, op0=ALU.min, op1=ALU.max
+                )
+            elif k >= SCALAR_RELU_FROM:
+                nc.scalar.activation(out=osb[:], in_=osb[:], func=ACT.Relu)
+            else:
+                nc.vector.tensor_scalar_max(out=osb[:], in0=osb[:], scalar1=0.0)
+            if c == 0:
+                nc.sync.dma_start(out=out[rows, 128:1152], in_=osb[:])
+            else:
+                nc.sync.dma_start(out=out[rows, 1152:2048], in_=osb[:, 0:896])
+                nc.sync.dma_start(out=out[rows, 0:128], in_=osb[:, 896:1024])
+
+        def on(k):
+            return 0 <= k < NCH
+
+        for s in range(NCH + 4):
+            if on(s + 2) and s + 2 >= 2:
+                load(s + 2)
+            if on(s - 3):
+                rg(s - 3)
+            if on(s):
+                tr(s)
+            if s == 0:
+                biases()
+            if on(s - 4):
+                yadd(s - 4)
+            if on(s - 1):
+                l1(s - 1)
+            if on(s - 3):
+                qh(s - 3)
+                l2(s - 3)
+            if on(s):
+                qx(s)

@@ -18,7 +18,7 @@ FLOPS = 2 * B * T * ((PK + F) * G + G * F)
 PINNED = True
 GPSIMD_RELU_BELOW = 0
 SCALAR_RELU_FROM = 99
-BT, BA, BY = 3, 3, 2
+BR, BY = 6, 2
 
 
 def tile_capsuleneuralnetwork_pa_t_kernel(tc, primary_input, prev, col, W0, b0, W1, b1, out):
@@ -115,7 +115,7 @@ def tile_capsuleneuralnetwork_pa_t_kernel(tc, primary_input, prev, col, W0, b0, 
             gxw = gx[:].bitcast(F32).rearrange("p (g n u) -> p g n u", g=2, u=2)
             for g in range(2):
                 for h in range(2):
-                    tp = psum.tile([P, 512], F32, tag="T", bufs=BT, name="tp")
+                    tp = psum.tile([P, 512], F32, tag="R", bufs=BR, name="tp")
                     tpv = tp[:].rearrange("p (t u b) -> p t u b", t=2, u=2)
                     for tt in range(2):
                         tl = 2 * h + tt
@@ -145,7 +145,7 @@ def tile_capsuleneuralnetwork_pa_t_kernel(tc, primary_input, prev, col, W0, b0, 
             htv = ht_t[i][:].rearrange("p (s n) -> p s n", s=4)
             xq, xs = xq_t[k], xs_t[k]
             for m in range(4):
-                acc = psum.tile([P, 512], F32, tag="A", bufs=BA, name="acc")
+                acc = psum.tile([P, 512], F32, tag="R", bufs=BR, name="acc")
                 for g in range(2):
                     wc = slice(G * g + P * m, G * g + P * m + P)
                     xc = slice(512 * g, 512 * g + 512)

@@ -16,7 +16,7 @@ B, T, PK, F, G = 1024, 8, 768, 256, 512
 NCH = 2 * (B // P)
 FLOPS = 2 * B * T * ((PK + F) * G + G * F)
 PINNED = True
-GPSIMD_RELU_BELOW = 0
+GPSIMD_RELU_BELOW = 14
 SCALAR_RELU_FROM = 99
 BR, BY = 6, 2
 
@@ -50,6 +50,9 @@ def tile_capsuleneuralnetwork_pa_t_kernel(tc, primary_input, prev, col, W0, b0, 
         )
         load(0)
         load(1)
+        load(2)
+        load(3)
+        load(4)
 
         c1 = const.tile([1, 1], BF16)
         nc.scalar.dma_start(out=c1[:], in_=col.rearrange("(a b) -> a b", a=1))
@@ -225,8 +228,8 @@ def tile_capsuleneuralnetwork_pa_t_kernel(tc, primary_input, prev, col, W0, b0, 
             return 0 <= k < NCH
 
         for s in range(NCH + 4):
-            if on(s + 2) and s + 2 >= 2:
-                load(s + 2)
+            if on(s + 5):
+                load(s + 5)
             if on(s - 3):
                 rg(s - 3)
             if on(s):

@@ -15,23 +15,23 @@ P = 128
 B, T, PK, F, G = 1024, 8, 768, 256, 512
 NCH = 2 * (B // P)
 FLOPS = 2 * B * T * ((PK + F) * G + G * F)
-PINNED = True
-GPSIMD_RELU_BELOW = 14
-SCALAR_RELU_FROM = 99
-BR, BY = 6, 2
+PREFETCH = 5
+RING, YBANKS = 6, 2
+VECTOR_X3 = [0,1,2,3,4,6,8,10,12]
+RG_ENGINE = {13:"G",15:"S"}
+RELU_ENGINE = {15:"V"}
 
 
 def tile_capsuleneuralnetwork_pa_t_kernel(tc, primary_input, prev, col, W0, b0, W1, b1, out):
     nc = tc.nc
     with ExitStack() as ctx:
-        if PINNED:
-            ctx.enter_context(tc.manual_schedule())
+        ctx.enter_context(tc.manual_schedule())
         const = ctx.enter_context(tc.tile_pool(name="const", bufs=1))
         xpool = ctx.enter_context(tc.tile_pool(name="xpool", bufs=8))
         work = ctx.enter_context(tc.tile_pool(name="work", bufs=3))
         psum = ctx.enter_context(tc.psum_pool(name="psum", bufs=1))
 
-        xp_t, xv_t, gx_t, xq_t, xs_t, ht_t, gh_t, hq_t, hs_t, y_t = {}, {}, {}, {}, {}, {}, {}, {}, {}, {}
+        xp_t, xv_t, gx_t, tp_t, xq_t, xs_t, ht_t, gh_t, hq_t, hs_t, y_t = {}, {}, {}, {}, {}, {}, {}, {}, {}, {}, {}
 
         def load(k):
             i, c = divmod(k, 2)
@@ -43,16 +43,12 @@ def tile_capsuleneuralnetwork_pa_t_kernel(tc, primary_input, prev, col, W0, b0, 
             xp_t[k], xv_t[k] = xp, xv
 
         w0raw = const.tile([P, 4 * 2 * G], BF16)
-
         nc.sync.dma_start(
             out=w0raw[:].rearrange("p (a r) -> p a r", a=4),
             in_=W0[0 : PK + F, :].rearrange("(a p e) n -> p a (e n)", a=4, e=2),
         )
-        load(0)
-        load(1)
-        load(2)
-        load(3)
-        load(4)
+        for k in range(PREFETCH):
+            load(k)
 
         c1 = const.tile([1, 1], BF16)
         nc.scalar.dma_start(out=c1[:], in_=col.rearrange("(a b) -> a b", a=1))
@@ -99,11 +95,11 @@ def tile_capsuleneuralnetwork_pa_t_kernel(tc, primary_input, prev, col, W0, b0, 
         bias0 = const.tile([P, 4], F32)
 
         def biases():
-            pb1 = psum.tile([P, 512], F32, tag="Y", bufs=BY, name="pb1")
+            pb1 = psum.tile([P, 512], F32, tag="Y", bufs=YBANKS, name="pb1")
             for r in range(2):
                 nc.tensor.matmul(out=pb1[:, F * r : F * (r + 1)], lhsT=colones[:], rhs=wb1[:], start=True, stop=True)
             nc.vector.tensor_copy(out=bias1[:], in_=pb1[:])
-            pb0 = psum.tile([P, 512], F32, tag="Y", bufs=BY, name="pb0")
+            pb0 = psum.tile([P, 512], F32, tag="Y", bufs=YBANKS, name="pb0")
             for m in range(4):
                 nc.tensor.matmul(
                     out=pb0[:, 32 * m : 32 * (m + 1)], lhsT=wb0[:, P * m : P * (m + 1)], rhs=colones[:, 0:32],
@@ -111,31 +107,40 @@ def tile_capsuleneuralnetwork_pa_t_kernel(tc, primary_input, prev, col, W0, b0, 
                 )
             nc.vector.tensor_copy(out=bias0[:], in_=pb0[:, 0:128].rearrange("p (m n) -> p m n", m=4)[:, :, 0])
 
+        def x_exit(k, bank, engine):
+            g, h = divmod(bank, 2)
+            gxw = gx_t[k][:].bitcast(F32).rearrange("p (g n u) -> p g n u", g=2, u=2)
+            dst = gxw[:, g, 256 * h : 256 * h + 256, :].rearrange("p (t b) u -> p t b u", t=2)
+            src = tp_t[(k, bank)][:].rearrange("p (t u b) -> p t b u", t=2, u=2)
+            if engine == "V":
+                nc.vector.tensor_copy(out=dst, in_=src)
+            else:
+                nc.scalar.copy(out=dst, in_=src)
+
         def tr(k):
             xpw = xp_t[k][:].bitcast(F32)
             xvw = xv_t[k][:].bitcast(F32)
-            gx = work.tile([P, 4096], BF16, tag="gx", name="gx", align_bytes=64)
-            gxw = gx[:].bitcast(F32).rearrange("p (g n u) -> p g n u", g=2, u=2)
-            for g in range(2):
-                for h in range(2):
-                    tp = psum.tile([P, 512], F32, tag="R", bufs=BR, name="tp")
-                    tpv = tp[:].rearrange("p (t u b) -> p t u b", t=2, u=2)
-                    for tt in range(2):
-                        tl = 2 * h + tt
-                        for u in range(2):
-                            if g == 1 and u == 1:
-                                src = xvw[:, 128 * tl : 128 * tl + 128]
-                            else:
-                                w = 384 * tl + 256 * g + 128 * u
-                                src = xpw[:, w : w + 128]
-                            nc.tensor.transpose(tpv[:, tt, u, :], src, ident[:])
-                    nc.scalar.copy(
-                        out=gxw[:, g, 256 * h : 256 * h + 256, :].rearrange("p (t b) u -> p t b u", t=2),
-                        in_=tpv.rearrange("p t u b -> p t b u"),
-                    )
-            gx_t[k] = gx
+            gx_t[k] = work.tile([P, 4096], BF16, tag="gx", name="gx", align_bytes=64)
+            for bank in range(4):
+                g, h = divmod(bank, 2)
+                tp = psum.tile([P, 512], F32, tag="R", bufs=RING, name="tp")
+                tp_t[(k, bank)] = tp
+                tpv = tp[:].rearrange("p (t u b) -> p t u b", t=2, u=2)
+                for tt in range(2):
+                    tl = 2 * h + tt
+                    for u in range(2):
+                        if g == 1 and u == 1:
+                            src = xvw[:, 128 * tl : 128 * tl + 128]
+                        else:
+                            w = 384 * tl + 256 * g + 128 * u
+                            src = xpw[:, w : w + 128]
+                        nc.tensor.transpose(tpv[:, tt, u, :], src, ident[:])
+                if bank < 3 or k not in VECTOR_X3:
+                    x_exit(k, bank, "S")
 
         def qx(k):
+            if k in VECTOR_X3:
+                x_exit(k, 3, "V")
             xq = work.tile([P, 1024], U32, tag="xq", name="xq", align_bytes=64)
             xs = work.tile([P, 1024], U8, tag="xs", name="xs", align_bytes=64)
             nc.vector.quantize_mx(out=xq[:].bitcast(FP8X4), scales=xs[:], in_=gx_t[k][:])
@@ -148,7 +153,7 @@ def tile_capsuleneuralnetwork_pa_t_kernel(tc, primary_input, prev, col, W0, b0, 
             htv = ht_t[i][:].rearrange("p (s n) -> p s n", s=4)
             xq, xs = xq_t[k], xs_t[k]
             for m in range(4):
-                acc = psum.tile([P, 512], F32, tag="R", bufs=BR, name="acc")
+                acc = psum.tile([P, 512], F32, tag="R", bufs=RING, name="acc")
                 for g in range(2):
                     wc = slice(G * g + P * m, G * g + P * m + P)
                     xc = slice(512 * g, 512 * g + 512)
@@ -172,12 +177,21 @@ def tile_capsuleneuralnetwork_pa_t_kernel(tc, primary_input, prev, col, W0, b0, 
 
         def rg(k):
             i, c = divmod(k, 2)
-            htv = ht_t[i][:].rearrange("p (s n) -> p s n", s=4)
+            hts = ht_t[i][:].rearrange("p (s n) -> p s n", s=4)[:, :, 512 * c : 512 * c + 512]
             gh = work.tile([P, 2048], BF16, tag="gh", name="gh", align_bytes=64)
-            nc.vector.tensor_copy(
-                out=gh[:].rearrange("p (c i s) -> p c s i", i=4, s=4),
-                in_=htv[:, :, 512 * c : 512 * c + 512].rearrange("p s (c i) -> p c s i", i=4),
-            )
+            engine = RG_ENGINE.get(k, "V")
+            if engine == "G":
+                nc.gpsimd.tensor_scalar(
+                    out=gh[:].rearrange("p (n s) -> p n s", s=4), in0=hts.rearrange("p s n -> p n s"),
+                    scalar1=1.0, scalar2=0.0, op0=ALU.mult, op1=ALU.add,
+                )
+            else:
+                dst = gh[:].rearrange("p (c i s) -> p c s i", i=4, s=4)
+                src = hts.rearrange("p s (c i) -> p c s i", i=4)
+                if engine == "S":
+                    nc.scalar.copy(out=dst, in_=src)
+                else:
+                    nc.vector.tensor_copy(out=dst, in_=src)
             gh_t[k] = gh
 
         def qh(k):
@@ -190,7 +204,7 @@ def tile_capsuleneuralnetwork_pa_t_kernel(tc, primary_input, prev, col, W0, b0, 
             hq, hs = hq_t[k], hs_t[k]
             ys = []
             for j in range(2):
-                y = psum.tile([P, 512], F32, tag="Y", bufs=BY, name="y")
+                y = psum.tile([P, 512], F32, tag="Y", bufs=YBANKS, name="y")
                 for tt in range(2):
                     hc = slice(P * (2 * j + tt), P * (2 * j + tt) + P)
                     nc.tensor.matmul_mx(
@@ -210,11 +224,12 @@ def tile_capsuleneuralnetwork_pa_t_kernel(tc, primary_input, prev, col, W0, b0, 
                 nc.vector.tensor_tensor(
                     out=osb[:, 512 * j : 512 * (j + 1)], in0=y_t[k][j][:], in1=bias1[:], op=ALU.add
                 )
-            if k < GPSIMD_RELU_BELOW:
+            engine = RELU_ENGINE.get(k, "G")
+            if engine == "G":
                 nc.gpsimd.tensor_scalar(
                     out=osb[:], in0=osb[:], scalar1=3.0e38, scalar2=0.0, op0=ALU.min, op1=ALU.max
                 )
-            elif k >= SCALAR_RELU_FROM:
+            elif engine == "S":
                 nc.scalar.activation(out=osb[:], in_=osb[:], func=ACT.Relu)
             else:
                 nc.vector.tensor_scalar_max(out=osb[:], in0=osb[:], scalar1=0.0)
@@ -228,9 +243,9 @@ def tile_capsuleneuralnetwork_pa_t_kernel(tc, primary_input, prev, col, W0, b0, 
             return 0 <= k < NCH
 
         for s in range(NCH + 4):
-            if on(s + 5):
-                load(s + 5)
-            if on(s - 3):
+            if on(s + PREFETCH):
+                load(s + PREFETCH)
+            if on(s - 3) and RG_ENGINE.get(s - 3, "V") != "S":
                 rg(s - 3)
             if on(s):
                 tr(s)
@@ -241,6 +256,8 @@ def tile_capsuleneuralnetwork_pa_t_kernel(tc, primary_input, prev, col, W0, b0, 
             if on(s - 1):
                 l1(s - 1)
             if on(s - 3):
+                if RG_ENGINE.get(s - 3, "V") == "S":
+                    rg(s - 3)
                 qh(s - 3)
                 l2(s - 3)
             if on(s):

@@ -17,9 +17,9 @@ NCH = 2 * (B // P)
 FLOPS = 2 * B * T * ((PK + F) * G + G * F)
 PREFETCH = 5
 RING, YBANKS = 6, 2
-VECTOR_X3 = [0,1,2,3,4,6,8,10,12]
-RG_ENGINE = {13:"G",15:"S"}
-RELU_ENGINE = {15:"V"}
+VECTOR_X3 = []
+RG_ENGINE = {}
+RELU_ENGINE = {14:"V",15:"V"}
 
 
 def tile_capsuleneuralnetwork_pa_t_kernel(tc, primary_input, prev, col, W0, b0, W1, b1, out):
@@ -242,11 +242,11 @@ def tile_capsuleneuralnetwork_pa_t_kernel(tc, primary_input, prev, col, W0, b0, 
         def on(k):
             return 0 <= k < NCH
 
-        for s in range(NCH + 4):
+        for s in range(NCH + 5):
             if on(s + PREFETCH):
                 load(s + PREFETCH)
-            if on(s - 3) and RG_ENGINE.get(s - 3, "V") != "S":
-                rg(s - 3)
+            if on(s - 3):
+                qh(s - 3)
             if on(s):
                 tr(s)
             if s == 0:
@@ -256,9 +256,8 @@ def tile_capsuleneuralnetwork_pa_t_kernel(tc, primary_input, prev, col, W0, b0, 
             if on(s - 1):
                 l1(s - 1)
             if on(s - 3):
-                if RG_ENGINE.get(s - 3, "V") == "S":
-                    rg(s - 3)
-                qh(s - 3)
                 l2(s - 3)
+            if on(s - 2):
+                rg(s - 2)
             if on(s):
                 qx(s)

@@ -12,14 +12,21 @@ ACT = mybir.ActivationFunctionType
 ALU = mybir.AluOpType
 
 P = 128
-B, T, PK, F, G = 1024, 8, 768, 256, 512
-NCH = 2 * (B // P)
-FLOPS = 2 * B * T * ((PK + F) * G + G * F)
+BATCH, CAPS, P_IN, X_IN, HID = 1024, 8, 768, 256, 512
+K1 = P_IN + X_IN
+CHUNK_CAPS = 4
+COLS = CHUNK_CAPS * P
+CHUNKS = BATCH // P * CAPS // CHUNK_CAPS
+BANK = 512
+ROLL = 128
+P_WORDS, X_WORDS = P_IN // 2, X_IN // 2
+Y_COLS = CHUNK_CAPS * X_IN
+FLOPS = 2 * BATCH * CAPS * (K1 * HID + HID * X_IN)
+
 PREFETCH = 5
-RING, YBANKS = 6, 2
-VECTOR_X3 = []
-RG_ENGINE = {}
-RELU_ENGINE = {14:"V",15:"V"}
+RING_BANKS = 6
+Y_BANKS = 2
+FLOAT32_MAX = 3.4028234663852886e38
 
 
 def tile_capsuleneuralnetwork_pa_t_kernel(tc, primary_input, prev, col, W0, b0, W1, b1, out):
@@ -31,233 +38,217 @@ def tile_capsuleneuralnetwork_pa_t_kernel(tc, primary_input, prev, col, W0, b0, 
         work = ctx.enter_context(tc.tile_pool(name="work", bufs=3))
         psum = ctx.enter_context(tc.psum_pool(name="psum", bufs=1))
 
-        xp_t, xv_t, gx_t, tp_t, xq_t, xs_t, ht_t, gh_t, hq_t, hs_t, y_t = {}, {}, {}, {}, {}, {}, {}, {}, {}, {}, {}
+        p_rows, x_rows, in_grouped, in_codes, in_scales = {}, {}, {}, {}, {}
+        relu_a, h_grouped, h_codes, h_scales, y_sums = {}, {}, {}, {}, {}
 
-        def load(k):
-            i, c = divmod(k, 2)
-            rows = slice(P * i, P * i + P)
-            xp = xpool.tile([P, 4 * PK], BF16, tag="xp", name="xp")
-            nc.sync.dma_start(out=xp[:], in_=primary_input[rows, 4 * PK * c : 4 * PK * (c + 1)])
-            xv = xpool.tile([P, 4 * F], BF16, tag="xv", name="xv")
-            nc.sync.dma_start(out=xv[:], in_=prev[rows, 4 * F * c : 4 * F * (c + 1)])
-            xp_t[k], xv_t[k] = xp, xv
+        def load(chunk):
+            tile_no, half = divmod(chunk, 2)
+            rows = slice(P * tile_no, P * tile_no + P)
+            xp = xpool.tile([P, CHUNK_CAPS * P_IN], BF16, tag="xp", name="xp")
+            nc.sync.dma_start(
+                out=xp[:], in_=primary_input[rows, CHUNK_CAPS * P_IN * half : CHUNK_CAPS * P_IN * (half + 1)]
+            )
+            xv = xpool.tile([P, CHUNK_CAPS * X_IN], BF16, tag="xv", name="xv")
+            nc.sync.dma_start(out=xv[:], in_=prev[rows, CHUNK_CAPS * X_IN * half : CHUNK_CAPS * X_IN * (half + 1)])
+            p_rows[chunk], x_rows[chunk] = xp, xv
 
-        w0raw = const.tile([P, 4 * 2 * G], BF16)
+        w0_rows = const.tile([P, 4 * 2 * HID], BF16)
         nc.sync.dma_start(
-            out=w0raw[:].rearrange("p (a r) -> p a r", a=4),
-            in_=W0[0 : PK + F, :].rearrange("(a p e) n -> p a (e n)", a=4, e=2),
+            out=w0_rows[:].rearrange("p (a r) -> p a r", a=4),
+            in_=W0[0:K1, :].rearrange("(a p e) n -> p a (e n)", a=4, e=2),
         )
-        for k in range(PREFETCH):
-            load(k)
+        for chunk in range(PREFETCH):
+            load(chunk)
 
-        c1 = const.tile([1, 1], BF16)
-        nc.scalar.dma_start(out=c1[:], in_=col.rearrange("(a b) -> a b", a=1))
-        wb0 = const.tile([P, G], BF16)
-        wb1 = const.tile([P, F], BF16)
-        colones = const.tile([P, P], BF16)
-        nc.vector.memset(wb0[:], 0.0)
-        nc.vector.memset(wb1[:], 0.0)
-        nc.vector.memset(colones[:], 0.0)
-        nc.vector.memset(colones[32:33, :], 1.0)
-        nc.scalar.dma_start(out=wb0[0:1, :], in_=W0[PK + F : PK + F + 1, :])
-        nc.scalar.dma_start(out=wb0[32:33, :], in_=b0.rearrange("(o n) -> o n", o=1))
-        nc.scalar.dma_start(out=wb1[0:1, :], in_=W1[G : G + 1, :])
-        nc.scalar.dma_start(out=wb1[32:33, :], in_=b1.rearrange("(o n) -> o n", o=1))
-        w1raw = const.tile([P, 4 * F], BF16)
+        col_sb = const.tile([1, 1], BF16)
+        nc.scalar.dma_start(out=col_sb[:], in_=col.rearrange("(a b) -> a b", a=1))
+        last0 = const.tile([P, HID], BF16)
+        last1 = const.tile([P, X_IN], BF16)
+        col_and_one = const.tile([P, P], BF16)
+        nc.vector.memset(last0[:], 0.0)
+        nc.vector.memset(last1[:], 0.0)
+        nc.vector.memset(col_and_one[:], 0.0)
+        nc.vector.memset(col_and_one[32:33, :], 1.0)
+        nc.scalar.dma_start(out=last0[0:1, :], in_=W0[K1 : K1 + 1, :])
+        nc.scalar.dma_start(out=last0[32:33, :], in_=b0.rearrange("(o n) -> o n", o=1))
+        nc.scalar.dma_start(out=last1[0:1, :], in_=W1[HID : HID + 1, :])
+        nc.scalar.dma_start(out=last1[32:33, :], in_=b1.rearrange("(o n) -> o n", o=1))
+        w1_rows = const.tile([P, 4 * X_IN], BF16)
         nc.scalar.dma_start(
-            out=w1raw[:].rearrange("p (s f) -> p s f", s=4),
-            in_=W1[0:G, :].rearrange("(s p) f -> p s f", p=P),
+            out=w1_rows[:].rearrange("p (s f) -> p s f", s=4),
+            in_=W1[0:HID, :].rearrange("(s p) f -> p s f", p=P),
         )
-        nc.vector.tensor_copy(out=colones[0:1, :], in_=c1[0:1, 0:1].to_broadcast([1, P]))
+        nc.vector.tensor_copy(out=col_and_one[0:1, :], in_=col_sb[0:1, 0:1].to_broadcast([1, P]))
 
-        ident = const.tile([P, P], F32)
-        make_identity(nc, ident[:])
+        identity = const.tile([P, P], F32)
+        make_identity(nc, identity[:])
 
-        w0g = const.tile([P, 2 * G * 4], BF16, align_bytes=64)
-        w0q = const.tile([P, 2 * G], U32, align_bytes=64)
-        w0s = const.tile([P, 2 * G], U8, align_bytes=64)
+        w0_grouped = const.tile([P, 2 * HID * 4], BF16, align_bytes=64)
+        w0_codes = const.tile([P, 2 * HID], U32, align_bytes=64)
+        w0_scales = const.tile([P, 2 * HID], U8, align_bytes=64)
         for g in range(2):
             nc.vector.tensor_copy(
-                out=w0g[:, 4 * G * g : 4 * G * (g + 1)].rearrange("p (c i t) -> p c t i", i=4, t=4),
-                in_=w0raw[:, 4 * G * g : 4 * G * (g + 1)].rearrange("p (t c i) -> p c t i", t=4, i=4),
+                out=w0_grouped[:, 4 * HID * g : 4 * HID * (g + 1)].rearrange("p (w i c) -> p w c i", i=4, c=4),
+                in_=w0_rows[:, 4 * HID * g : 4 * HID * (g + 1)].rearrange("p (c w i) -> p w c i", c=4, i=4),
             )
-        w1g = const.tile([P, F * 4], BF16, align_bytes=64)
-        w1q = const.tile([P, F], U32, align_bytes=64)
-        w1s = const.tile([P, F], U8, align_bytes=64)
+        w1_grouped = const.tile([P, X_IN * 4], BF16, align_bytes=64)
+        w1_codes = const.tile([P, X_IN], U32, align_bytes=64)
+        w1_scales = const.tile([P, X_IN], U8, align_bytes=64)
         nc.vector.tensor_copy(
-            out=w1g[:].rearrange("p (c i t) -> p c t i", i=4, t=4),
-            in_=w1raw[:].rearrange("p (t c i) -> p c t i", t=4, i=4),
+            out=w1_grouped[:].rearrange("p (w i c) -> p w c i", i=4, c=4),
+            in_=w1_rows[:].rearrange("p (c w i) -> p w c i", c=4, i=4),
         )
-        nc.vector.quantize_mx(out=w0q[:].bitcast(FP8X4), scales=w0s[:], in_=w0g[:])
-        nc.vector.quantize_mx(out=w1q[:].bitcast(FP8X4), scales=w1s[:], in_=w1g[:])
+        nc.vector.quantize_mx(out=w0_codes[:].bitcast(FP8X4), scales=w0_scales[:], in_=w0_grouped[:])
+        nc.vector.quantize_mx(out=w1_codes[:].bitcast(FP8X4), scales=w1_scales[:], in_=w1_grouped[:])
 
-        bias1 = const.tile([P, 2 * F], F32)
+        bias1 = const.tile([P, 2 * X_IN], F32)
         bias0 = const.tile([P, 4], F32)
 
         def biases():
-            pb1 = psum.tile([P, 512], F32, tag="Y", bufs=YBANKS, name="pb1")
+            spread = psum.tile([P, BANK], F32, tag="Y", bufs=Y_BANKS, name="pb1")
             for r in range(2):
-                nc.tensor.matmul(out=pb1[:, F * r : F * (r + 1)], lhsT=colones[:], rhs=wb1[:], start=True, stop=True)
-            nc.vector.tensor_copy(out=bias1[:], in_=pb1[:])
-            pb0 = psum.tile([P, 512], F32, tag="Y", bufs=YBANKS, name="pb0")
-            for m in range(4):
                 nc.tensor.matmul(
-                    out=pb0[:, 32 * m : 32 * (m + 1)], lhsT=wb0[:, P * m : P * (m + 1)], rhs=colones[:, 0:32],
-                    start=True, stop=True,
+                    out=spread[:, X_IN * r : X_IN * (r + 1)], lhsT=col_and_one[:], rhs=last1[:], start=True, stop=True
                 )
-            nc.vector.tensor_copy(out=bias0[:], in_=pb0[:, 0:128].rearrange("p (m n) -> p m n", m=4)[:, :, 0])
+            nc.vector.tensor_copy(out=bias1[:], in_=spread[:])
+            upright = psum.tile([P, BANK], F32, tag="Y", bufs=Y_BANKS, name="pb0")
+            for block in range(4):
+                nc.tensor.matmul(
+                    out=upright[:, 32 * block : 32 * (block + 1)], lhsT=last0[:, P * block : P * (block + 1)],
+                    rhs=col_and_one[:, 0:32], start=True, stop=True,
+                )
+            nc.vector.tensor_copy(out=bias0[:], in_=upright[:, 0 : 4 * 32].rearrange("p (m n) -> p m n", m=4)[:, :, 0])
 
-        def x_exit(k, bank, engine):
-            g, h = divmod(bank, 2)
-            gxw = gx_t[k][:].bitcast(F32).rearrange("p (g n u) -> p g n u", g=2, u=2)
-            dst = gxw[:, g, 256 * h : 256 * h + 256, :].rearrange("p (t b) u -> p t b u", t=2)
-            src = tp_t[(k, bank)][:].rearrange("p (t u b) -> p t b u", t=2, u=2)
-            if engine == "V":
-                nc.vector.tensor_copy(out=dst, in_=src)
-            else:
-                nc.scalar.copy(out=dst, in_=src)
+        def transpose_input(chunk):
+            p_words = p_rows[chunk][:].bitcast(F32)
+            x_words = x_rows[chunk][:].bitcast(F32)
+            grouped = work.tile([P, 2 * COLS * 4], BF16, tag="gx", name="gx", align_bytes=64)
+            grouped_words = grouped[:].bitcast(F32).rearrange("p (g n u) -> p g n u", g=2, u=2)
+            for g in range(2):
+                for pair in range(2):
+                    bank = psum.tile([P, BANK], F32, tag="R", bufs=RING_BANKS, name="tp")
+                    bank_view = bank[:].rearrange("p (t u b) -> p t u b", t=2, u=2)
+                    for t in range(2):
+                        cap = 2 * pair + t
+                        for u in range(2):
+                            if g == 1 and u == 1:
+                                words = x_words[:, X_WORDS * cap : X_WORDS * cap + P]
+                            else:
+                                first = P_WORDS * cap + 2 * P * g + P * u
+                                words = p_words[:, first : first + P]
+                            nc.tensor.transpose(bank_view[:, t, u, :], words, identity[:])
+                    two_caps = grouped_words[:, g, 2 * P * pair : 2 * P * (pair + 1), :]
+                    nc.scalar.copy(
+                        out=two_caps.rearrange("p (t b) u -> p t b u", t=2),
+                        in_=bank_view.rearrange("p t u b -> p t b u"),
+                    )
+            in_grouped[chunk] = grouped
 
-        def tr(k):
-            xpw = xp_t[k][:].bitcast(F32)
-            xvw = xv_t[k][:].bitcast(F32)
-            gx_t[k] = work.tile([P, 4096], BF16, tag="gx", name="gx", align_bytes=64)
-            for bank in range(4):
-                g, h = divmod(bank, 2)
-                tp = psum.tile([P, 512], F32, tag="R", bufs=RING, name="tp")
-                tp_t[(k, bank)] = tp
-                tpv = tp[:].rearrange("p (t u b) -> p t u b", t=2, u=2)
-                for tt in range(2):
-                    tl = 2 * h + tt
-                    for u in range(2):
-                        if g == 1 and u == 1:
-                            src = xvw[:, 128 * tl : 128 * tl + 128]
-                        else:
-                            w = 384 * tl + 256 * g + 128 * u
-                            src = xpw[:, w : w + 128]
-                        nc.tensor.transpose(tpv[:, tt, u, :], src, ident[:])
-                if bank < 3 or k not in VECTOR_X3:
-                    x_exit(k, bank, "S")
+        def quantise_input(chunk):
+            codes = work.tile([P, 2 * COLS], U32, tag="xq", name="xq", align_bytes=64)
+            scales = work.tile([P, 2 * COLS], U8, tag="xs", name="xs", align_bytes=64)
+            nc.vector.quantize_mx(out=codes[:].bitcast(FP8X4), scales=scales[:], in_=in_grouped[chunk][:])
+            in_codes[chunk], in_scales[chunk] = codes, scales
 
-        def qx(k):
-            if k in VECTOR_X3:
-                x_exit(k, 3, "V")
-            xq = work.tile([P, 1024], U32, tag="xq", name="xq", align_bytes=64)
-            xs = work.tile([P, 1024], U8, tag="xs", name="xs", align_bytes=64)
-            nc.vector.quantize_mx(out=xq[:].bitcast(FP8X4), scales=xs[:], in_=gx_t[k][:])
-            xq_t[k], xs_t[k] = xq, xs
-
-        def l1(k):
-            i, c = divmod(k, 2)
-            if c == 0:
-                ht_t[i] = work.tile([P, 4096], BF16, tag="ht", name="ht")
-            htv = ht_t[i][:].rearrange("p (s n) -> p s n", s=4)
-            xq, xs = xq_t[k], xs_t[k]
-            for m in range(4):
-                acc = psum.tile([P, 512], F32, tag="R", bufs=RING, name="acc")
+        def layer1(chunk):
+            tile_no, half = divmod(chunk, 2)
+            if half == 0:
+                relu_a[tile_no] = work.tile([P, 4 * 2 * COLS], BF16, tag="ht", name="ht")
+            slots = relu_a[tile_no][:].rearrange("p (s n) -> p s n", s=4)
+            codes, scales = in_codes[chunk], in_scales[chunk]
+            for block in range(4):
+                sums = psum.tile([P, BANK], F32, tag="R", bufs=RING_BANKS, name="acc")
                 for g in range(2):
-                    wc = slice(G * g + P * m, G * g + P * m + P)
-                    xc = slice(512 * g, 512 * g + 512)
+                    w_cols = slice(HID * g + P * block, HID * g + P * block + P)
+                    in_cols = slice(COLS * g, COLS * g + COLS)
                     nc.tensor.matmul_mx(
-                        out=acc[:],
-                        lhsT=w0q[:, wc].bitcast(FP8X4), lhsT_scale=w0s[:, wc],
-                        rhs=xq[:, xc].bitcast(FP8X4), rhs_scale=xs[:, xc],
+                        out=sums[:],
+                        lhsT=w0_codes[:, w_cols].bitcast(FP8X4), lhsT_scale=w0_scales[:, w_cols],
+                        rhs=codes[:, in_cols].bitcast(FP8X4), rhs_scale=scales[:, in_cols],
                         start=(g == 0), stop=(g == 1),
                     )
-                bias = bias0[:, m : m + 1]
-                if m > 0:
-                    pieces = [(0, 512, m - 1, 512 * c)]
-                elif c == 0:
-                    pieces = [(0, 128, 3, 896), (128, 512, 3, 0)]
+                if block > 0:
+                    pieces = [(0, COLS, block - 1, COLS * half)]
+                elif half == 0:
+                    pieces = [(0, P, 3, 7 * P), (P, COLS, 3, 0)]
                 else:
-                    pieces = [(0, 512, 3, 384)]
-                for lo, hi, s, dst in pieces:
+                    pieces = [(0, COLS, 3, COLS - P)]
+                for lo, hi, slot, dst in pieces:
                     nc.scalar.activation(
-                        out=htv[:, s, dst : dst + hi - lo], in_=acc[:, lo:hi], func=ACT.Relu, bias=bias, scale=1.0
+                        out=slots[:, slot, dst : dst + hi - lo], in_=sums[:, lo:hi], func=ACT.Relu,
+                        bias=bias0[:, block : block + 1], scale=1.0,
                     )
 
-        def rg(k):
-            i, c = divmod(k, 2)
-            hts = ht_t[i][:].rearrange("p (s n) -> p s n", s=4)[:, :, 512 * c : 512 * c + 512]
-            gh = work.tile([P, 2048], BF16, tag="gh", name="gh", align_bytes=64)
-            engine = RG_ENGINE.get(k, "V")
-            if engine == "G":
-                nc.gpsimd.tensor_scalar(
-                    out=gh[:].rearrange("p (n s) -> p n s", s=4), in0=hts.rearrange("p s n -> p n s"),
-                    scalar1=1.0, scalar2=0.0, op0=ALU.mult, op1=ALU.add,
-                )
-            else:
-                dst = gh[:].rearrange("p (c i s) -> p c s i", i=4, s=4)
-                src = hts.rearrange("p s (c i) -> p c s i", i=4)
-                if engine == "S":
-                    nc.scalar.copy(out=dst, in_=src)
-                else:
-                    nc.vector.tensor_copy(out=dst, in_=src)
-            gh_t[k] = gh
+        def regroup_h(chunk):
+            tile_no, half = divmod(chunk, 2)
+            slots = relu_a[tile_no][:].rearrange("p (s n) -> p s n", s=4)
+            grouped = work.tile([P, COLS * 4], BF16, tag="gh", name="gh", align_bytes=64)
+            nc.vector.tensor_copy(
+                out=grouped[:].rearrange("p (w i s) -> p w s i", i=4, s=4),
+                in_=slots[:, :, COLS * half : COLS * half + COLS].rearrange("p s (w i) -> p w s i", i=4),
+            )
+            h_grouped[chunk] = grouped
 
-        def qh(k):
-            hq = work.tile([P, 512], U32, tag="hq", name="hq", align_bytes=64)
-            hs = work.tile([P, 512], U8, tag="hs", name="hs", align_bytes=64)
-            nc.vector.quantize_mx(out=hq[:].bitcast(FP8X4), scales=hs[:], in_=gh_t[k][:])
-            hq_t[k], hs_t[k] = hq, hs
+        def quantise_h(chunk):
+            codes = work.tile([P, COLS], U32, tag="hq", name="hq", align_bytes=64)
+            scales = work.tile([P, COLS], U8, tag="hs", name="hs", align_bytes=64)
+            nc.vector.quantize_mx(out=codes[:].bitcast(FP8X4), scales=scales[:], in_=h_grouped[chunk][:])
+            h_codes[chunk], h_scales[chunk] = codes, scales
 
-        def l2(k):
-            hq, hs = hq_t[k], hs_t[k]
-            ys = []
-            for j in range(2):
-                y = psum.tile([P, 512], F32, tag="Y", bufs=YBANKS, name="y")
-                for tt in range(2):
-                    hc = slice(P * (2 * j + tt), P * (2 * j + tt) + P)
+        def layer2(chunk):
+            codes, scales = h_codes[chunk], h_scales[chunk]
+            banks = []
+            for pair in range(2):
+                sums = psum.tile([P, BANK], F32, tag="Y", bufs=Y_BANKS, name="y")
+                for t in range(2):
+                    rows = slice(P * (2 * pair + t), P * (2 * pair + t) + P)
                     nc.tensor.matmul_mx(
-                        out=y[:, F * tt : F * (tt + 1)],
-                        lhsT=hq[:, hc].bitcast(FP8X4), lhsT_scale=hs[:, hc],
-                        rhs=w1q[:].bitcast(FP8X4), rhs_scale=w1s[:],
+                        out=sums[:, X_IN * t : X_IN * (t + 1)],
+                        lhsT=codes[:, rows].bitcast(FP8X4), lhsT_scale=scales[:, rows],
+                        rhs=w1_codes[:].bitcast(FP8X4), rhs_scale=w1_scales[:],
                         start=True, stop=True,
                     )
-                ys.append(y)
-            y_t[k] = ys
+                banks.append(sums)
+            y_sums[chunk] = banks
 
-        def yadd(k):
-            i, c = divmod(k, 2)
-            rows = slice(P * i, P * i + P)
-            osb = work.tile([P, 1024], F32, tag="osb", bufs=4, name="osb")
-            for j in range(2):
+        def finish(chunk):
+            tile_no, half = divmod(chunk, 2)
+            rows = slice(P * tile_no, P * tile_no + P)
+            result = work.tile([P, Y_COLS], F32, tag="osb", bufs=4, name="osb")
+            for pair in range(2):
                 nc.vector.tensor_tensor(
-                    out=osb[:, 512 * j : 512 * (j + 1)], in0=y_t[k][j][:], in1=bias1[:], op=ALU.add
+                    out=result[:, BANK * pair : BANK * (pair + 1)], in0=y_sums[chunk][pair][:], in1=bias1[:], op=ALU.add
                 )
-            engine = RELU_ENGINE.get(k, "G")
-            if engine == "G":
+            if chunk < CHUNKS - 2:
                 nc.gpsimd.tensor_scalar(
-                    out=osb[:], in0=osb[:], scalar1=3.0e38, scalar2=0.0, op0=ALU.min, op1=ALU.max
+                    out=result[:], in0=result[:], scalar1=FLOAT32_MAX, scalar2=0.0, op0=ALU.min, op1=ALU.max
                 )
-            elif engine == "S":
-                nc.scalar.activation(out=osb[:], in_=osb[:], func=ACT.Relu)
             else:
-                nc.vector.tensor_scalar_max(out=osb[:], in0=osb[:], scalar1=0.0)
-            if c == 0:
-                nc.sync.dma_start(out=out[rows, 128:1152], in_=osb[:])
+                nc.vector.tensor_scalar_max(out=result[:], in0=result[:], scalar1=0.0)
+            if half == 0:
+                nc.sync.dma_start(out=out[rows, ROLL : ROLL + Y_COLS], in_=result[:])
             else:
-                nc.sync.dma_start(out=out[rows, 1152:2048], in_=osb[:, 0:896])
-                nc.sync.dma_start(out=out[rows, 0:128], in_=osb[:, 896:1024])
+                nc.sync.dma_start(out=out[rows, ROLL + Y_COLS : 2 * Y_COLS], in_=result[:, 0 : Y_COLS - ROLL])
+                nc.sync.dma_start(out=out[rows, 0:ROLL], in_=result[:, Y_COLS - ROLL : Y_COLS])
 
-        def on(k):
-            return 0 <= k < NCH
+        def exists(chunk):
+            return 0 <= chunk < CHUNKS
 
-        for s in range(NCH + 5):
-            if on(s + PREFETCH):
-                load(s + PREFETCH)
-            if on(s - 3):
-                qh(s - 3)
-            if on(s):
-                tr(s)
-            if s == 0:
+        for step in range(CHUNKS + 4):
+            if exists(step + PREFETCH):
+                load(step + PREFETCH)
+            if exists(step - 3):
+                regroup_h(step - 3)
+            if exists(step):
+                transpose_input(step)
+            if step == 0:
                 biases()
-            if on(s - 4):
-                yadd(s - 4)
-            if on(s - 1):
-                l1(s - 1)
-            if on(s - 3):
-                l2(s - 3)
-            if on(s - 2):
-                rg(s - 2)
-            if on(s):
-                qx(s)
+            if exists(step - 4):
+                finish(step - 4)
+            if exists(step - 1):
+                layer1(step - 1)
+            if exists(step - 3):
+                quantise_h(step - 3)
+                layer2(step - 3)
+            if exists(step):
+                quantise_input(step)

from contextlib import ExitStack

import concourse.mybir as mybir
from concourse.masks import make_identity

F32 = mybir.dt.float32
BF16 = mybir.dt.bfloat16
U32 = mybir.dt.uint32
U8 = mybir.dt.uint8
FP8X4 = mybir.dt.float8_e4m3fn_x4
ACT = mybir.ActivationFunctionType
ALU = mybir.AluOpType

P = 128
BATCH, CAPS, P_IN, X_IN, HID = 1024, 8, 768, 256, 512
K1 = P_IN + X_IN
CHUNK_CAPS = 4
COLS = CHUNK_CAPS * P
CHUNKS = BATCH // P * CAPS // CHUNK_CAPS
BANK = 512
ROLL = 128
P_WORDS, X_WORDS = P_IN // 2, X_IN // 2
Y_COLS = CHUNK_CAPS * X_IN
FLOPS = 2 * BATCH * CAPS * (K1 * HID + HID * X_IN)

PREFETCH = 5
RING_BANKS = 6
Y_BANKS = 2
FLOAT32_MAX = 3.4028234663852886e38


def tile_capsuleneuralnetwork_pa_t_kernel(tc, primary_input, prev, col, W0, b0, W1, b1, out):
    nc = tc.nc
    with ExitStack() as ctx:
        ctx.enter_context(tc.manual_schedule())
        const = ctx.enter_context(tc.tile_pool(name="const", bufs=1))
        xpool = ctx.enter_context(tc.tile_pool(name="xpool", bufs=8))
        work = ctx.enter_context(tc.tile_pool(name="work", bufs=3))
        psum = ctx.enter_context(tc.psum_pool(name="psum", bufs=1))

        p_rows, x_rows, in_grouped, in_codes, in_scales = {}, {}, {}, {}, {}
        relu_a, h_grouped, h_codes, h_scales, y_sums = {}, {}, {}, {}, {}

        def load(chunk):
            tile_no, half = divmod(chunk, 2)
            rows = slice(P * tile_no, P * tile_no + P)
            xp = xpool.tile([P, CHUNK_CAPS * P_IN], BF16, tag="xp", name="xp")
            nc.sync.dma_start(
                out=xp[:], in_=primary_input[rows, CHUNK_CAPS * P_IN * half : CHUNK_CAPS * P_IN * (half + 1)]
            )
            xv = xpool.tile([P, CHUNK_CAPS * X_IN], BF16, tag="xv", name="xv")
            nc.sync.dma_start(out=xv[:], in_=prev[rows, CHUNK_CAPS * X_IN * half : CHUNK_CAPS * X_IN * (half + 1)])
            p_rows[chunk], x_rows[chunk] = xp, xv

        w0_rows = const.tile([P, 4 * 2 * HID], BF16)
        nc.sync.dma_start(
            out=w0_rows[:].rearrange("p (a r) -> p a r", a=4),
            in_=W0[0:K1, :].rearrange("(a p e) n -> p a (e n)", a=4, e=2),
        )
        for chunk in range(PREFETCH):
            load(chunk)

        col_sb = const.tile([1, 1], BF16)
        nc.scalar.dma_start(out=col_sb[:], in_=col.rearrange("(a b) -> a b", a=1))
        last0 = const.tile([P, HID], BF16)
        last1 = const.tile([P, X_IN], BF16)
        col_and_one = const.tile([P, P], BF16)
        nc.vector.memset(last0[:], 0.0)
        nc.vector.memset(last1[:], 0.0)
        nc.vector.memset(col_and_one[:], 0.0)
        nc.vector.memset(col_and_one[32:33, :], 1.0)
        nc.scalar.dma_start(out=last0[0:1, :], in_=W0[K1 : K1 + 1, :])
        nc.scalar.dma_start(out=last0[32:33, :], in_=b0.rearrange("(o n) -> o n", o=1))
        nc.scalar.dma_start(out=last1[0:1, :], in_=W1[HID : HID + 1, :])
        nc.scalar.dma_start(out=last1[32:33, :], in_=b1.rearrange("(o n) -> o n", o=1))
        w1_rows = const.tile([P, 4 * X_IN], BF16)
        nc.scalar.dma_start(
            out=w1_rows[:].rearrange("p (s f) -> p s f", s=4),
            in_=W1[0:HID, :].rearrange("(s p) f -> p s f", p=P),
        )
        nc.vector.tensor_copy(out=col_and_one[0:1, :], in_=col_sb[0:1, 0:1].to_broadcast([1, P]))

        identity = const.tile([P, P], F32)
        make_identity(nc, identity[:])

        w0_grouped = const.tile([P, 2 * HID * 4], BF16, align_bytes=64)
        w0_codes = const.tile([P, 2 * HID], U32, align_bytes=64)
        w0_scales = const.tile([P, 2 * HID], U8, align_bytes=64)
        for g in range(2):
            nc.vector.tensor_copy(
                out=w0_grouped[:, 4 * HID * g : 4 * HID * (g + 1)].rearrange("p (w i c) -> p w c i", i=4, c=4),
                in_=w0_rows[:, 4 * HID * g : 4 * HID * (g + 1)].rearrange("p (c w i) -> p w c i", c=4, i=4),
            )
        w1_grouped = const.tile([P, X_IN * 4], BF16, align_bytes=64)
        w1_codes = const.tile([P, X_IN], U32, align_bytes=64)
        w1_scales = const.tile([P, X_IN], U8, align_bytes=64)
        nc.vector.tensor_copy(
            out=w1_grouped[:].rearrange("p (w i c) -> p w c i", i=4, c=4),
            in_=w1_rows[:].rearrange("p (c w i) -> p w c i", c=4, i=4),
        )
        nc.vector.quantize_mx(out=w0_codes[:].bitcast(FP8X4), scales=w0_scales[:], in_=w0_grouped[:])
        nc.vector.quantize_mx(out=w1_codes[:].bitcast(FP8X4), scales=w1_scales[:], in_=w1_grouped[:])

        bias1 = const.tile([P, 2 * X_IN], F32)
        bias0 = const.tile([P, 4], F32)

        def biases():
            spread = psum.tile([P, BANK], F32, tag="Y", bufs=Y_BANKS, name="pb1")
            for r in range(2):
                nc.tensor.matmul(
                    out=spread[:, X_IN * r : X_IN * (r + 1)], lhsT=col_and_one[:], rhs=last1[:], start=True, stop=True
                )
            nc.vector.tensor_copy(out=bias1[:], in_=spread[:])
            upright = psum.tile([P, BANK], F32, tag="Y", bufs=Y_BANKS, name="pb0")
            for block in range(4):
                nc.tensor.matmul(
                    out=upright[:, 32 * block : 32 * (block + 1)], lhsT=last0[:, P * block : P * (block + 1)],
                    rhs=col_and_one[:, 0:32], start=True, stop=True,
                )
            nc.vector.tensor_copy(out=bias0[:], in_=upright[:, 0 : 4 * 32].rearrange("p (m n) -> p m n", m=4)[:, :, 0])

        def transpose_input(chunk):
            p_words = p_rows[chunk][:].bitcast(F32)
            x_words = x_rows[chunk][:].bitcast(F32)
            grouped = work.tile([P, 2 * COLS * 4], BF16, tag="gx", name="gx", align_bytes=64)
            grouped_words = grouped[:].bitcast(F32).rearrange("p (g n u) -> p g n u", g=2, u=2)
            for g in range(2):
                for pair in range(2):
                    bank = psum.tile([P, BANK], F32, tag="R", bufs=RING_BANKS, name="tp")
                    bank_view = bank[:].rearrange("p (t u b) -> p t u b", t=2, u=2)
                    for t in range(2):
                        cap = 2 * pair + t
                        for u in range(2):
                            if g == 1 and u == 1:
                                words = x_words[:, X_WORDS * cap : X_WORDS * cap + P]
                            else:
                                first = P_WORDS * cap + 2 * P * g + P * u
                                words = p_words[:, first : first + P]
                            nc.tensor.transpose(bank_view[:, t, u, :], words, identity[:])
                    two_caps = grouped_words[:, g, 2 * P * pair : 2 * P * (pair + 1), :]
                    nc.scalar.copy(
                        out=two_caps.rearrange("p (t b) u -> p t b u", t=2),
                        in_=bank_view.rearrange("p t u b -> p t b u"),
                    )
            in_grouped[chunk] = grouped

        def quantise_input(chunk):
            codes = work.tile([P, 2 * COLS], U32, tag="xq", name="xq", align_bytes=64)
            scales = work.tile([P, 2 * COLS], U8, tag="xs", name="xs", align_bytes=64)
            nc.vector.quantize_mx(out=codes[:].bitcast(FP8X4), scales=scales[:], in_=in_grouped[chunk][:])
            in_codes[chunk], in_scales[chunk] = codes, scales

        def layer1(chunk):
            tile_no, half = divmod(chunk, 2)
            if half == 0:
                relu_a[tile_no] = work.tile([P, 4 * 2 * COLS], BF16, tag="ht", name="ht")
            slots = relu_a[tile_no][:].rearrange("p (s n) -> p s n", s=4)
            codes, scales = in_codes[chunk], in_scales[chunk]
            for block in range(4):
                sums = psum.tile([P, BANK], F32, tag="R", bufs=RING_BANKS, name="acc")
                for g in range(2):
                    w_cols = slice(HID * g + P * block, HID * g + P * block + P)
                    in_cols = slice(COLS * g, COLS * g + COLS)
                    nc.tensor.matmul_mx(
                        out=sums[:],
                        lhsT=w0_codes[:, w_cols].bitcast(FP8X4), lhsT_scale=w0_scales[:, w_cols],
                        rhs=codes[:, in_cols].bitcast(FP8X4), rhs_scale=scales[:, in_cols],
                        start=(g == 0), stop=(g == 1),
                    )
                if block > 0:
                    pieces = [(0, COLS, block - 1, COLS * half)]
                elif half == 0:
                    pieces = [(0, P, 3, 7 * P), (P, COLS, 3, 0)]
                else:
                    pieces = [(0, COLS, 3, COLS - P)]
                for lo, hi, slot, dst in pieces:
                    nc.scalar.activation(
                        out=slots[:, slot, dst : dst + hi - lo], in_=sums[:, lo:hi], func=ACT.Relu,
                        bias=bias0[:, block : block + 1], scale=1.0,
                    )

        def regroup_h(chunk):
            tile_no, half = divmod(chunk, 2)
            slots = relu_a[tile_no][:].rearrange("p (s n) -> p s n", s=4)
            grouped = work.tile([P, COLS * 4], BF16, tag="gh", name="gh", align_bytes=64)
            nc.vector.tensor_copy(
                out=grouped[:].rearrange("p (w i s) -> p w s i", i=4, s=4),
                in_=slots[:, :, COLS * half : COLS * half + COLS].rearrange("p s (w i) -> p w s i", i=4),
            )
            h_grouped[chunk] = grouped

        def quantise_h(chunk):
            codes = work.tile([P, COLS], U32, tag="hq", name="hq", align_bytes=64)
            scales = work.tile([P, COLS], U8, tag="hs", name="hs", align_bytes=64)
            nc.vector.quantize_mx(out=codes[:].bitcast(FP8X4), scales=scales[:], in_=h_grouped[chunk][:])
            h_codes[chunk], h_scales[chunk] = codes, scales

        def layer2(chunk):
            codes, scales = h_codes[chunk], h_scales[chunk]
            banks = []
            for pair in range(2):
                sums = psum.tile([P, BANK], F32, tag="Y", bufs=Y_BANKS, name="y")
                for t in range(2):
                    rows = slice(P * (2 * pair + t), P * (2 * pair + t) + P)
                    nc.tensor.matmul_mx(
                        out=sums[:, X_IN * t : X_IN * (t + 1)],
                        lhsT=codes[:, rows].bitcast(FP8X4), lhsT_scale=scales[:, rows],
                        rhs=w1_codes[:].bitcast(FP8X4), rhs_scale=w1_scales[:],
                        start=True, stop=True,
                    )
                banks.append(sums)
            y_sums[chunk] = banks

        def finish(chunk):
            tile_no, half = divmod(chunk, 2)
            rows = slice(P * tile_no, P * tile_no + P)
            result = work.tile([P, Y_COLS], F32, tag="osb", bufs=4, name="osb")
            for pair in range(2):
                nc.vector.tensor_tensor(
                    out=result[:, BANK * pair : BANK * (pair + 1)], in0=y_sums[chunk][pair][:], in1=bias1[:], op=ALU.add
                )
            if chunk < CHUNKS - 2:
                nc.gpsimd.tensor_scalar(
                    out=result[:], in0=result[:], scalar1=FLOAT32_MAX, scalar2=0.0, op0=ALU.min, op1=ALU.max
                )
            else:
                nc.vector.tensor_scalar_max(out=result[:], in0=result[:], scalar1=0.0)
            if half == 0:
                nc.sync.dma_start(out=out[rows, ROLL : ROLL + Y_COLS], in_=result[:])
            else:
                nc.sync.dma_start(out=out[rows, ROLL + Y_COLS : 2 * Y_COLS], in_=result[:, 0 : Y_COLS - ROLL])
                nc.sync.dma_start(out=out[rows, 0:ROLL], in_=result[:, Y_COLS - ROLL : Y_COLS])

        def exists(chunk):
            return 0 <= chunk < CHUNKS

        for step in range(CHUNKS + 4):
            if exists(step + PREFETCH):
                load(step + PREFETCH)
            if exists(step - 3):
                regroup_h(step - 3)
            if exists(step):
                transpose_input(step)
            if step == 0:
                biases()
            if exists(step - 4):
                finish(step - 4)
            if exists(step - 1):
                layer1(step - 1)
            if exists(step - 3):
                quantise_h(step - 3)
                layer2(step - 3)
            if exists(step):
                quantise_input(step)
